import numpy as np
import ml_dtypes

BF16 = ml_dtypes.bfloat16


def bf(x):
    return np.asarray(x, np.float32).astype(BF16)


def f32(x):
    return np.asarray(x, np.float32)


def f64(x):
    return np.asarray(x).astype(np.float64)


def striped(idx):
    return np.tile(idx.reshape(-1, 16).T, (8, 1))


C, S, N = 512, 2048, 512
EPS = 1e-5


def setup_inputs():
    return {"tok_emb": f32(np.random.standard_normal((C, S))), "pos_emb": f32(np.random.standard_normal((C, N))), "lnf_w": f32(1.0 + 0.1 * np.random.standard_normal((C, 1))), "lnf_b": f32(0.1 * np.random.standard_normal((C, 1))), "head_w": bf(np.random.standard_normal((C, S)) / np.sqrt(C)), "offs": striped(np.random.permutation(np.tile(np.arange(S), 2))[:N])}


def reference(tok_emb, pos_emb, lnf_w, lnf_b, head_w, offs):
    idx = offs[:16].T.reshape(-1)
    h = f64(tok_emb)[:, idx] + f64(pos_emb)
    mu = h.mean(axis=0, keepdims=True)
    var = np.square(h - mu).mean(axis=0, keepdims=True)
    hn = (h - mu) / np.sqrt(var + EPS) * f64(lnf_w) + f64(lnf_b)
    return f64(head_w).T @ hn

@@ -1,0 +1,86 @@
+import concourse.mybir as mybir
+
+P = 128
+C, S, N = 512, 2048, 512
+CB = C // P
+VB = S // P
+EPS = 1e-5
+FLOPS = 2 * C * S * N
+
+F32, BF16, U16 = mybir.dt.float32, mybir.dt.bfloat16, mybir.dt.uint16
+ADD, SUBTRACT, MULT = mybir.AluOpType.add, mybir.AluOpType.subtract, mybir.AluOpType.mult
+SQUARE = mybir.ActivationFunctionType.Square
+SQRT = mybir.ActivationFunctionType.Sqrt
+IDENTITY = mybir.ActivationFunctionType.Identity
+COPY = mybir.ActivationFunctionType.Copy
+
+
+def tile_tinygpt_ntp_kernel(tc, tok_emb, pos_emb, lnf_w, lnf_b, head_w, offs, out):
+    nc = tc.nc
+    with (
+        tc.tile_pool(name="held", bufs=1) as held,
+        tc.tile_pool(name="work", bufs=2) as work,
+        tc.tile_pool(name="stage", bufs=4) as stage,
+        tc.psum_pool(name="psum", bufs=8) as psum,
+    ):
+        offsets = held.tile([P, N // 16], U16, name="offsets")
+        nc.sync.dma_start(offsets[:], offs)
+        tok = [held.tile([P, S], F32, name=f"tok{cb}") for cb in range(CB)]
+        pos = [held.tile([P, N], F32, name=f"pos{cb}") for cb in range(CB)]
+        head = [held.tile([P, S], BF16, name=f"head{cb}") for cb in range(CB)]
+        for cb in range(CB):
+            nc.sync.dma_start(tok[cb][:], tok_emb[cb * P : (cb + 1) * P, :])
+            nc.sync.dma_start(pos[cb][:], pos_emb[cb * P : (cb + 1) * P, :])
+        gain = held.tile([P, CB], F32, name="gain")
+        bias = held.tile([P, CB], F32, name="bias")
+        with nc.allow_non_contiguous_dma(reason="512 single values, one to a partition"):
+            nc.sync.dma_start(gain[:], lnf_w.rearrange("(cb p) one -> p (cb one)", p=P))
+            nc.sync.dma_start(bias[:], lnf_b.rearrange("(cb p) one -> p (cb one)", p=P))
+        for cb in range(CB):
+            nc.sync.dma_start(head[cb][:], head_w[cb * P : (cb + 1) * P, :])
+
+        averager = held.tile([P, P], F32, name="averager")
+        nc.vector.memset(averager[:], 1.0 / C)
+        eps = held.tile([P, 1], F32, name="eps")
+        nc.vector.memset(eps[:], EPS)
+
+        mean = psum.tile([P, N], F32, name="mean", tag="bank")
+        h = [held.tile([P, N], F32, name=f"h{cb}") for cb in range(CB)]
+        for cb in range(CB):
+            nc.vector.tensor_tensor(h[cb][:], tok[cb][:].indirect(offsets[:]), pos[cb][:], ADD)
+            nc.tensor.matmul(mean[:], averager[:], h[cb][:], start=(cb == 0), stop=(cb == CB - 1))
+
+        variance = psum.tile([P, N], F32, name="variance", tag="bank")
+        centred = [held.tile([P, N], F32, name=f"centred{cb}") for cb in range(CB)]
+        for cb in range(CB):
+            nc.vector.tensor_tensor(centred[cb][:], h[cb][:], mean[:], SUBTRACT)
+            squared = work.tile([P, N], F32, name="squared")
+            nc.scalar.activation(squared[:], centred[cb][:], SQUARE)
+            nc.tensor.matmul(variance[:], averager[:], squared[:], start=(cb == 0), stop=(cb == CB - 1))
+
+        std = held.tile([P, N], F32, name="std")
+        nc.scalar.activation(std[:], variance[:], SQRT, bias=eps[:])
+        rstd = held.tile([P, N], F32, name="rstd")
+        nc.vector.reciprocal(rstd[:], std[:])
+
+        hn = [held.tile([P, N], BF16, name=f"hn{cb}") for cb in range(CB)]
+        for cb in range(CB):
+            unit = work.tile([P, N], F32, name="unit")
+            nc.vector.tensor_tensor(unit[:], centred[cb][:], rstd[:], MULT)
+            nc.scalar.activation(
+                hn[cb][:], unit[:], IDENTITY, bias=bias[:, cb : cb + 1], scale=gain[:, cb : cb + 1]
+            )
+
+        for vb in range(VB):
+            logits = psum.tile([P, N], F32, name="logits", tag="bank")
+            for cb in range(CB):
+                nc.tensor.matmul(
+                    logits[:], head[cb][:, vb * P : (vb + 1) * P], hn[cb][:],
+                    start=(cb == 0), stop=(cb == CB - 1),
+                )
+            staged = stage.tile([P, N], F32, name="staged")
+            if vb % 2 == 0:
+                nc.vector.tensor_copy(staged[:], logits[:])
+            else:
+                nc.scalar.activation(staged[:], logits[:], COPY)
+            nc.sync.dma_start(out[vb * P : (vb + 1) * P, :], staged[:])

@@ -10,7 +10,7 @@ FLOPS = 2 * C * S * N
 F32, BF16, U16 = mybir.dt.float32, mybir.dt.bfloat16, mybir.dt.uint16
 ADD, SUBTRACT, MULT = mybir.AluOpType.add, mybir.AluOpType.subtract, mybir.AluOpType.mult
 SQUARE = mybir.ActivationFunctionType.Square
-SQRT = mybir.ActivationFunctionType.Sqrt
+RSQRT = mybir.ActivationFunctionType.Abs_reciprocal_sqrt
 IDENTITY = mybir.ActivationFunctionType.Identity
 COPY = mybir.ActivationFunctionType.Copy
 
@@ -58,10 +58,8 @@ def tile_tinygpt_ntp_kernel(tc, tok_emb, pos_emb, lnf_w, lnf_b, head_w, offs, ou
             nc.scalar.activation(squared[:], centred[cb][:], SQUARE)
             nc.tensor.matmul(variance[:], averager[:], squared[:], start=(cb == 0), stop=(cb == CB - 1))
 
-        std = held.tile([P, N], F32, name="std")
-        nc.scalar.activation(std[:], variance[:], SQRT, bias=eps[:])
         rstd = held.tile([P, N], F32, name="rstd")
-        nc.vector.reciprocal(rstd[:], std[:])
+        nc.scalar.activation(rstd[:], variance[:], RSQRT, bias=eps[:])
 
         hn = [held.tile([P, N], BF16, name=f"hn{cb}") for cb in range(CB)]
         for cb in range(CB):

@@ -4,6 +4,7 @@ P = 128
 C, S, N = 512, 2048, 512
 CB = C // P
 VB = S // P
+GROUP = 4
 EPS = 1e-5
 FLOPS = 2 * C * S * N
 
@@ -29,38 +30,59 @@ def tile_tinygpt_ntp_kernel(tc, tok_emb, pos_emb, lnf_w, lnf_b, head_w, offs, ou
         pos = [held.tile([P, N], F32, name=f"pos{cb}") for cb in range(CB)]
         head = [held.tile([P, S], BF16, name=f"head{cb}") for cb in range(CB)]
         for cb in range(CB):
-            nc.sync.dma_start(tok[cb][:], tok_emb[cb * P : (cb + 1) * P, :])
             nc.sync.dma_start(pos[cb][:], pos_emb[cb * P : (cb + 1) * P, :])
+            nc.sync.dma_start(tok[cb][:], tok_emb[cb * P : (cb + 1) * P, :])
+        for cb in range(CB):
+            nc.sync.dma_start(head[cb][:], head_w[cb * P : (cb + 1) * P, :])
         gain = held.tile([P, CB], F32, name="gain")
         bias = held.tile([P, CB], F32, name="bias")
         with nc.allow_non_contiguous_dma(reason="512 single values, one to a partition"):
-            nc.sync.dma_start(gain[:], lnf_w.rearrange("(cb p) one -> p (cb one)", p=P))
-            nc.sync.dma_start(bias[:], lnf_b.rearrange("(cb p) one -> p (cb one)", p=P))
-        for cb in range(CB):
-            nc.sync.dma_start(head[cb][:], head_w[cb * P : (cb + 1) * P, :])
+            nc.scalar.dma_start(gain[:], lnf_w.rearrange("(cb p) one -> p (cb one)", p=P))
+            nc.scalar.dma_start(bias[:], lnf_b.rearrange("(cb p) one -> p (cb one)", p=P))
 
+        block_averager = held.tile([P, P], F32, name="block_averager")
+        nc.vector.memset(block_averager[:], 1.0 / P)
         averager = held.tile([P, P], F32, name="averager")
         nc.vector.memset(averager[:], 1.0 / C)
         eps = held.tile([P, 1], F32, name="eps")
         nc.vector.memset(eps[:], EPS)
+        table_warmer = held.tile([P, 1], F32, name="table_warmer")
+        nc.scalar.activation(table_warmer[:], eps[:], RSQRT)
 
-        mean = psum.tile([P, N], F32, name="mean", tag="bank")
-        h = [held.tile([P, N], F32, name=f"h{cb}") for cb in range(CB)]
+        shift = psum.tile([P, N], F32, name="shift", tag="bank")
+        delta = psum.tile([P, N], F32, name="delta", tag="bank")
+        e = [held.tile([P, N], F32, name=f"e{cb}") for cb in range(CB)]
+        squares = held.tile([P, N], F32, name="squares")
         for cb in range(CB):
-            nc.vector.tensor_tensor(h[cb][:], tok[cb][:].indirect(offsets[:]), pos[cb][:], ADD)
-            nc.tensor.matmul(mean[:], averager[:], h[cb][:], start=(cb == 0), stop=(cb == CB - 1))
+            if cb == 0:
+                h0 = held.tile([P, N], F32, name="h0")
+                nc.vector.tensor_tensor(h0[:], tok[0][:].indirect(offsets[:]), pos[0][:], ADD)
+                nc.tensor.matmul(shift[:], block_averager[:], h0[:], start=True, stop=True)
+                nc.vector.tensor_tensor(e[0][:], h0[:], shift[:], SUBTRACT)
+                nc.scalar.activation(squares[:], e[0][:], SQUARE)
+            else:
+                shifted_pos = work.tile([P, N], F32, name="shifted_pos")
+                nc.vector.tensor_tensor(shifted_pos[:], pos[cb][:], shift[:], SUBTRACT)
+                nc.vector.tensor_tensor(
+                    e[cb][:], tok[cb][:].indirect(offsets[:]), shifted_pos[:], ADD
+                )
+                squared = work.tile([P, N], F32, name="squared")
+                nc.scalar.activation(squared[:], e[cb][:], SQUARE)
+                nc.vector.tensor_tensor(squares[:], squares[:], squared[:], ADD)
+            nc.tensor.matmul(delta[:], averager[:], e[cb][:], start=(cb == 0), stop=(cb == CB - 1))
+        spread = psum.tile([P, N], F32, name="spread", tag="bank")
+        nc.tensor.matmul(spread[:], averager[:], squares[:], start=True, stop=True)
 
-        variance = psum.tile([P, N], F32, name="variance", tag="bank")
-        centred = [held.tile([P, N], F32, name=f"centred{cb}") for cb in range(CB)]
-        for cb in range(CB):
-            nc.vector.tensor_tensor(centred[cb][:], h[cb][:], mean[:], SUBTRACT)
-            squared = work.tile([P, N], F32, name="squared")
-            nc.scalar.activation(squared[:], centred[cb][:], SQUARE)
-            nc.tensor.matmul(variance[:], averager[:], squared[:], start=(cb == 0), stop=(cb == CB - 1))
-
+        delta_squared = held.tile([P, N], F32, name="delta_squared")
+        nc.scalar.activation(delta_squared[:], delta[:], SQUARE)
+        variance = held.tile([P, N], F32, name="variance")
+        nc.vector.tensor_tensor(variance[:], spread[:], delta_squared[:], SUBTRACT)
         rstd = held.tile([P, N], F32, name="rstd")
         nc.scalar.activation(rstd[:], variance[:], RSQRT, bias=eps[:])
 
+        centred = [held.tile([P, N], F32, name=f"centred{cb}") for cb in range(CB)]
+        for cb in range(CB):
+            nc.vector.tensor_tensor(centred[cb][:], e[cb][:], delta[:], SUBTRACT)
         hn = [held.tile([P, N], BF16, name=f"hn{cb}") for cb in range(CB)]
         for cb in range(CB):
             unit = work.tile([P, N], F32, name="unit")
@@ -69,16 +91,19 @@ def tile_tinygpt_ntp_kernel(tc, tok_emb, pos_emb, lnf_w, lnf_b, head_w, offs, ou
                 hn[cb][:], unit[:], IDENTITY, bias=bias[:, cb : cb + 1], scale=gain[:, cb : cb + 1]
             )
 
-        for vb in range(VB):
-            logits = psum.tile([P, N], F32, name="logits", tag="bank")
+        for group in range(VB // GROUP):
+            blocks = range(group * GROUP, (group + 1) * GROUP)
+            logits = {vb: psum.tile([P, N], F32, name=f"logits{vb}", tag="bank") for vb in blocks}
             for cb in range(CB):
-                nc.tensor.matmul(
-                    logits[:], head[cb][:, vb * P : (vb + 1) * P], hn[cb][:],
-                    start=(cb == 0), stop=(cb == CB - 1),
-                )
-            staged = stage.tile([P, N], F32, name="staged")
-            if vb % 2 == 0:
-                nc.vector.tensor_copy(staged[:], logits[:])
-            else:
-                nc.scalar.activation(staged[:], logits[:], COPY)
-            nc.sync.dma_start(out[vb * P : (vb + 1) * P, :], staged[:])
+                for vb in blocks:
+                    nc.tensor.matmul(
+                        logits[vb][:], head[cb][:, vb * P : (vb + 1) * P], hn[cb][:],
+                        start=(cb == 0), stop=(cb == CB - 1),
+                    )
+            for vb in blocks:
+                staged = stage.tile([P, N], F32, name="staged")
+                if vb % 2 == 0:
+                    nc.vector.tensor_copy(staged[:], logits[vb][:])
+                else:
+                    nc.scalar.activation(staged[:], logits[vb][:], COPY)
+                nc.sync.dma_start(out[vb * P : (vb + 1) * P, :], staged[:])

@@ -5,6 +5,7 @@ C, S, N = 512, 2048, 512
 CB = C // P
 VB = S // P
 GROUP = 4
+EARLY = 2
 EPS = 1e-5
 FLOPS = 2 * C * S * N
 
@@ -27,18 +28,22 @@ def tile_tinygpt_ntp_kernel(tc, tok_emb, pos_emb, lnf_w, lnf_b, head_w, offs, ou
         offsets = held.tile([P, N // 16], U16, name="offsets")
         nc.sync.dma_start(offsets[:], offs)
         tok = [held.tile([P, S], F32, name=f"tok{cb}") for cb in range(CB)]
-        pos = [held.tile([P, N], F32, name=f"pos{cb}") for cb in range(CB)]
-        head = [held.tile([P, S], BF16, name=f"head{cb}") for cb in range(CB)]
-        for cb in range(CB):
-            nc.sync.dma_start(pos[cb][:], pos_emb[cb * P : (cb + 1) * P, :])
-            nc.sync.dma_start(tok[cb][:], tok_emb[cb * P : (cb + 1) * P, :])
-        for cb in range(CB):
-            nc.sync.dma_start(head[cb][:], head_w[cb * P : (cb + 1) * P, :])
+        pos_all = held.tile([P, CB, N], F32, name="pos_all")
+        head_all = held.tile([P, CB, S], BF16, name="head_all")
+        tok_blocks = tok_emb.rearrange("(p cb) s -> cb p s", cb=CB)
+        pos_blocks = pos_emb.rearrange("(p cb) j -> p cb j", cb=CB)
+        nc.sync.dma_start(pos_all[:, 0:1, :], pos_blocks[:, 0:1, :])
+        nc.sync.dma_start(tok[0][:], tok_blocks[0])
+        nc.sync.dma_start(pos_all[:, 1:CB, :], pos_blocks[:, 1:CB, :])
+        for cb in range(1, CB):
+            nc.sync.dma_start(tok[cb][:], tok_blocks[cb])
+        nc.sync.dma_start(head_all[:], head_w.rearrange("(p cb) v -> p cb v", cb=CB))
+        pos = [pos_all[:, cb, :] for cb in range(CB)]
+        head = [head_all[:, cb, :] for cb in range(CB)]
         gain = held.tile([P, CB], F32, name="gain")
         bias = held.tile([P, CB], F32, name="bias")
-        with nc.allow_non_contiguous_dma(reason="512 single values, one to a partition"):
-            nc.scalar.dma_start(gain[:], lnf_w.rearrange("(cb p) one -> p (cb one)", p=P))
-            nc.scalar.dma_start(bias[:], lnf_b.rearrange("(cb p) one -> p (cb one)", p=P))
+        nc.sync.dma_start(gain[:], lnf_w.rearrange("(p cb) one -> p (cb one)", cb=CB))
+        nc.sync.dma_start(bias[:], lnf_b.rearrange("(p cb) one -> p (cb one)", cb=CB))
 
         block_averager = held.tile([P, P], F32, name="block_averager")
         nc.vector.memset(block_averager[:], 1.0 / P)
@@ -52,47 +57,59 @@ def tile_tinygpt_ntp_kernel(tc, tok_emb, pos_emb, lnf_w, lnf_b, head_w, offs, ou
         shift = psum.tile([P, N], F32, name="shift", tag="bank")
         delta = psum.tile([P, N], F32, name="delta", tag="bank")
         e = [held.tile([P, N], F32, name=f"e{cb}") for cb in range(CB)]
+        h = [held.tile([P, N], F32, name=f"h{cb}") for cb in range(EARLY)]
+        for cb in range(EARLY):
+            nc.vector.tensor_tensor(h[cb][:], tok[cb][:].indirect(offsets[:]), pos[cb], ADD)
+        nc.tensor.matmul(shift[:], block_averager[:], h[0][:], start=True, stop=True)
         squares = held.tile([P, N], F32, name="squares")
         for cb in range(CB):
-            if cb == 0:
-                h0 = held.tile([P, N], F32, name="h0")
-                nc.vector.tensor_tensor(h0[:], tok[0][:].indirect(offsets[:]), pos[0][:], ADD)
-                nc.tensor.matmul(shift[:], block_averager[:], h0[:], start=True, stop=True)
-                nc.vector.tensor_tensor(e[0][:], h0[:], shift[:], SUBTRACT)
-                nc.scalar.activation(squares[:], e[0][:], SQUARE)
+            if cb < EARLY:
+                nc.vector.tensor_tensor(e[cb][:], h[cb][:], shift[:], SUBTRACT)
             else:
                 shifted_pos = work.tile([P, N], F32, name="shifted_pos")
-                nc.vector.tensor_tensor(shifted_pos[:], pos[cb][:], shift[:], SUBTRACT)
+                nc.vector.tensor_tensor(shifted_pos[:], pos[cb], shift[:], SUBTRACT)
                 nc.vector.tensor_tensor(
                     e[cb][:], tok[cb][:].indirect(offsets[:]), shifted_pos[:], ADD
                 )
+            nc.tensor.matmul(delta[:], averager[:], e[cb][:], start=(cb == 0), stop=(cb == CB - 1))
+            if cb == 0:
+                nc.scalar.activation(squares[:], e[0][:], SQUARE)
+            else:
                 squared = work.tile([P, N], F32, name="squared")
                 nc.scalar.activation(squared[:], e[cb][:], SQUARE)
                 nc.vector.tensor_tensor(squares[:], squares[:], squared[:], ADD)
-            nc.tensor.matmul(delta[:], averager[:], e[cb][:], start=(cb == 0), stop=(cb == CB - 1))
         spread = psum.tile([P, N], F32, name="spread", tag="bank")
         nc.tensor.matmul(spread[:], averager[:], squares[:], start=True, stop=True)
+
+        idle_work = psum.tile([P, N], F32, name="idle_work", tag="bank")
+
+        def keep_tensor_engine_busy(result):
+            nc.tensor.matmul(
+                idle_work[:, 0 : N // 2], averager[:], result[:, 0 : N // 2], start=True, stop=True
+            )
 
         delta_squared = held.tile([P, N], F32, name="delta_squared")
         nc.scalar.activation(delta_squared[:], delta[:], SQUARE)
         variance = held.tile([P, N], F32, name="variance")
         nc.vector.tensor_tensor(variance[:], spread[:], delta_squared[:], SUBTRACT)
+        keep_tensor_engine_busy(variance)
         rstd = held.tile([P, N], F32, name="rstd")
         nc.scalar.activation(rstd[:], variance[:], RSQRT, bias=eps[:])
+        keep_tensor_engine_busy(rstd)
 
-        centred = [held.tile([P, N], F32, name=f"centred{cb}") for cb in range(CB)]
-        for cb in range(CB):
-            nc.vector.tensor_tensor(centred[cb][:], e[cb][:], delta[:], SUBTRACT)
         hn = [held.tile([P, N], BF16, name=f"hn{cb}") for cb in range(CB)]
         for cb in range(CB):
+            centred = work.tile([P, N], F32, name="centred", bufs=CB)
+            nc.vector.tensor_tensor(centred[:], e[cb][:], delta[:], SUBTRACT)
             unit = work.tile([P, N], F32, name="unit")
-            nc.vector.tensor_tensor(unit[:], centred[cb][:], rstd[:], MULT)
+            nc.vector.tensor_tensor(unit[:], centred[:], rstd[:], MULT)
+            if cb == 0:
+                keep_tensor_engine_busy(unit)
             nc.scalar.activation(
                 hn[cb][:], unit[:], IDENTITY, bias=bias[:, cb : cb + 1], scale=gain[:, cb : cb + 1]
             )
 
-        for group in range(VB // GROUP):
-            blocks = range(group * GROUP, (group + 1) * GROUP)
+        for blocks in [range(GROUP)] + [range(vb, vb + 1) for vb in range(GROUP, VB)]:
             logits = {vb: psum.tile([P, N], F32, name=f"logits{vb}", tag="bank") for vb in blocks}
             for cb in range(CB):
                 for vb in blocks:

@@ -5,7 +5,6 @@ C, S, N = 512, 2048, 512
 CB = C // P
 VB = S // P
 GROUP = 4
-EARLY = 2
 EPS = 1e-5
 FLOPS = 2 * C * S * N
 
@@ -28,25 +27,21 @@ def tile_tinygpt_ntp_kernel(tc, tok_emb, pos_emb, lnf_w, lnf_b, head_w, offs, ou
         offsets = held.tile([P, N // 16], U16, name="offsets")
         nc.sync.dma_start(offsets[:], offs)
         tok = [held.tile([P, S], F32, name=f"tok{cb}") for cb in range(CB)]
-        pos_all = held.tile([P, CB, N], F32, name="pos_all")
-        head_all = held.tile([P, CB, S], BF16, name="head_all")
+        pos = held.tile([P, CB, N], F32, name="pos")
+        head = held.tile([P, CB, S], BF16, name="head")
         tok_blocks = tok_emb.rearrange("(p cb) s -> cb p s", cb=CB)
         pos_blocks = pos_emb.rearrange("(p cb) j -> p cb j", cb=CB)
-        nc.sync.dma_start(pos_all[:, 0:1, :], pos_blocks[:, 0:1, :])
+        nc.sync.dma_start(pos[:, 0:1, :], pos_blocks[:, 0:1, :])
         nc.sync.dma_start(tok[0][:], tok_blocks[0])
-        nc.sync.dma_start(pos_all[:, 1:CB, :], pos_blocks[:, 1:CB, :])
+        nc.sync.dma_start(pos[:, 1:CB, :], pos_blocks[:, 1:CB, :])
         for cb in range(1, CB):
             nc.sync.dma_start(tok[cb][:], tok_blocks[cb])
-        nc.sync.dma_start(head_all[:], head_w.rearrange("(p cb) v -> p cb v", cb=CB))
-        pos = [pos_all[:, cb, :] for cb in range(CB)]
-        head = [head_all[:, cb, :] for cb in range(CB)]
+        nc.sync.dma_start(head[:], head_w.rearrange("(p cb) v -> p cb v", cb=CB))
         gain = held.tile([P, CB], F32, name="gain")
         bias = held.tile([P, CB], F32, name="bias")
         nc.sync.dma_start(gain[:], lnf_w.rearrange("(p cb) one -> p (cb one)", cb=CB))
         nc.sync.dma_start(bias[:], lnf_b.rearrange("(p cb) one -> p (cb one)", cb=CB))
 
-        block_averager = held.tile([P, P], F32, name="block_averager")
-        nc.vector.memset(block_averager[:], 1.0 / P)
         averager = held.tile([P, P], F32, name="averager")
         nc.vector.memset(averager[:], 1.0 / C)
         eps = held.tile([P, 1], F32, name="eps")
@@ -54,32 +49,22 @@ def tile_tinygpt_ntp_kernel(tc, tok_emb, pos_emb, lnf_w, lnf_b, head_w, offs, ou
         table_warmer = held.tile([P, 1], F32, name="table_warmer")
         nc.scalar.activation(table_warmer[:], eps[:], RSQRT)
 
-        shift = psum.tile([P, N], F32, name="shift", tag="bank")
-        delta = psum.tile([P, N], F32, name="delta", tag="bank")
-        e = [held.tile([P, N], F32, name=f"e{cb}") for cb in range(CB)]
-        h = [held.tile([P, N], F32, name=f"h{cb}") for cb in range(EARLY)]
-        for cb in range(EARLY):
-            nc.vector.tensor_tensor(h[cb][:], tok[cb][:].indirect(offsets[:]), pos[cb], ADD)
-        nc.tensor.matmul(shift[:], block_averager[:], h[0][:], start=True, stop=True)
-        squares = held.tile([P, N], F32, name="squares")
+        mean = psum.tile([P, N], F32, name="mean", tag="bank")
+        h = [held.tile([P, N], F32, name=f"h{cb}") for cb in range(CB)]
         for cb in range(CB):
-            if cb < EARLY:
-                nc.vector.tensor_tensor(e[cb][:], h[cb][:], shift[:], SUBTRACT)
-            else:
-                shifted_pos = work.tile([P, N], F32, name="shifted_pos")
-                nc.vector.tensor_tensor(shifted_pos[:], pos[cb], shift[:], SUBTRACT)
-                nc.vector.tensor_tensor(
-                    e[cb][:], tok[cb][:].indirect(offsets[:]), shifted_pos[:], ADD
-                )
-            nc.tensor.matmul(delta[:], averager[:], e[cb][:], start=(cb == 0), stop=(cb == CB - 1))
-            if cb == 0:
-                nc.scalar.activation(squares[:], e[0][:], SQUARE)
-            else:
-                squared = work.tile([P, N], F32, name="squared")
-                nc.scalar.activation(squared[:], e[cb][:], SQUARE)
-                nc.vector.tensor_tensor(squares[:], squares[:], squared[:], ADD)
-        spread = psum.tile([P, N], F32, name="spread", tag="bank")
-        nc.tensor.matmul(spread[:], averager[:], squares[:], start=True, stop=True)
+            nc.vector.tensor_tensor(h[cb][:], tok[cb][:].indirect(offsets[:]), pos[:, cb, :], ADD)
+            nc.tensor.matmul(mean[:], averager[:], h[cb][:], start=(cb == 0), stop=(cb == CB - 1))
+
+        variance = psum.tile([P, N], F32, name="variance", tag="bank")
+        centred = [held.tile([P, N], F32, name=f"centred{cb}") for cb in range(CB)]
+        squared = [held.tile([P, N], F32, name=f"squared{cb}") for cb in range(CB)]
+        for cb in range(CB):
+            nc.vector.tensor_tensor(centred[cb][:], h[cb][:], mean[:], SUBTRACT)
+            nc.scalar.activation(squared[cb][:], centred[cb][:], SQUARE)
+        for cb in range(0, CB, 2):
+            pair = work.tile([P, N], F32, name="pair")
+            nc.vector.tensor_tensor(pair[:], squared[cb][:], squared[cb + 1][:], ADD)
+            nc.tensor.matmul(variance[:], averager[:], pair[:], start=(cb == 0), stop=(cb == CB - 2))
 
         idle_work = psum.tile([P, N], F32, name="idle_work", tag="bank")
 
@@ -88,21 +73,14 @@ def tile_tinygpt_ntp_kernel(tc, tok_emb, pos_emb, lnf_w, lnf_b, head_w, offs, ou
                 idle_work[:, 0 : N // 2], averager[:], result[:, 0 : N // 2], start=True, stop=True
             )
 
-        delta_squared = held.tile([P, N], F32, name="delta_squared")
-        nc.scalar.activation(delta_squared[:], delta[:], SQUARE)
-        variance = held.tile([P, N], F32, name="variance")
-        nc.vector.tensor_tensor(variance[:], spread[:], delta_squared[:], SUBTRACT)
-        keep_tensor_engine_busy(variance)
         rstd = held.tile([P, N], F32, name="rstd")
         nc.scalar.activation(rstd[:], variance[:], RSQRT, bias=eps[:])
         keep_tensor_engine_busy(rstd)
 
         hn = [held.tile([P, N], BF16, name=f"hn{cb}") for cb in range(CB)]
         for cb in range(CB):
-            centred = work.tile([P, N], F32, name="centred", bufs=CB)
-            nc.vector.tensor_tensor(centred[:], e[cb][:], delta[:], SUBTRACT)
             unit = work.tile([P, N], F32, name="unit")
-            nc.vector.tensor_tensor(unit[:], centred[:], rstd[:], MULT)
+            nc.vector.tensor_tensor(unit[:], centred[cb][:], rstd[:], MULT)
             if cb == 0:
                 keep_tensor_engine_busy(unit)
             nc.scalar.activation(
@@ -114,7 +92,7 @@ def tile_tinygpt_ntp_kernel(tc, tok_emb, pos_emb, lnf_w, lnf_b, head_w, offs, ou
             for cb in range(CB):
                 for vb in blocks:
                     nc.tensor.matmul(
-                        logits[vb][:], head[cb][:, vb * P : (vb + 1) * P], hn[cb][:],
+                        logits[vb][:], head[:, cb, vb * P : (vb + 1) * P], hn[cb][:],
                         start=(cb == 0), stop=(cb == CB - 1),
                     )
             for vb in blocks:

@@ -5,6 +5,8 @@ C, S, N = 512, 2048, 512
 CB = C // P
 VB = S // P
 GROUP = 4
+HALVES = (slice(0, N // 2), slice(N // 2, N))
+WHOLE = slice(0, N)
 EPS = 1e-5
 FLOPS = 2 * C * S * N
 
@@ -49,56 +51,58 @@ def tile_tinygpt_ntp_kernel(tc, tok_emb, pos_emb, lnf_w, lnf_b, head_w, offs, ou
         table_warmer = held.tile([P, 1], F32, name="table_warmer")
         nc.scalar.activation(table_warmer[:], eps[:], RSQRT)
 
-        mean = psum.tile([P, N], F32, name="mean", tag="bank")
+        mean = [psum.tile([P, N // 2], F32, name=f"mean{half}", tag="bank") for half in range(2)]
         h = [held.tile([P, N], F32, name=f"h{cb}") for cb in range(CB)]
         for cb in range(CB):
-            nc.vector.tensor_tensor(h[cb][:], tok[cb][:].indirect(offsets[:]), pos[:, cb, :], ADD)
-            nc.tensor.matmul(mean[:], averager[:], h[cb][:], start=(cb == 0), stop=(cb == CB - 1))
+            for half, cols in enumerate(HALVES):
+                entries = offsets[:, half * (N // 32) : (half + 1) * (N // 32)]
+                nc.vector.tensor_tensor(
+                    h[cb][:, cols], tok[cb][:].indirect(entries), pos[:, cb, cols], ADD
+                )
+                nc.tensor.matmul(
+                    mean[half][:], averager[:], h[cb][:, cols], start=(cb == 0), stop=(cb == CB - 1)
+                )
 
-        variance = psum.tile([P, N], F32, name="variance", tag="bank")
         centred = [held.tile([P, N], F32, name=f"centred{cb}") for cb in range(CB)]
         squared = [held.tile([P, N], F32, name=f"squared{cb}") for cb in range(CB)]
-        for cb in range(CB):
-            nc.vector.tensor_tensor(centred[cb][:], h[cb][:], mean[:], SUBTRACT)
-            nc.scalar.activation(squared[cb][:], centred[cb][:], SQUARE)
-        for cb in range(0, CB, 2):
-            pair = work.tile([P, N], F32, name="pair")
-            nc.vector.tensor_tensor(pair[:], squared[cb][:], squared[cb + 1][:], ADD)
-            nc.tensor.matmul(variance[:], averager[:], pair[:], start=(cb == 0), stop=(cb == CB - 2))
-
-        idle_work = psum.tile([P, N], F32, name="idle_work", tag="bank")
-
-        def keep_tensor_engine_busy(result):
-            nc.tensor.matmul(
-                idle_work[:, 0 : N // 2], averager[:], result[:, 0 : N // 2], start=True, stop=True
-            )
-
         rstd = held.tile([P, N], F32, name="rstd")
-        nc.scalar.activation(rstd[:], variance[:], RSQRT, bias=eps[:])
-        keep_tensor_engine_busy(rstd)
-
         hn = [held.tile([P, N], BF16, name=f"hn{cb}") for cb in range(CB)]
-        for cb in range(CB):
-            unit = work.tile([P, N], F32, name="unit")
-            nc.vector.tensor_tensor(unit[:], centred[cb][:], rstd[:], MULT)
-            if cb == 0:
-                keep_tensor_engine_busy(unit)
-            nc.scalar.activation(
-                hn[cb][:], unit[:], IDENTITY, bias=bias[:, cb : cb + 1], scale=gain[:, cb : cb + 1]
-            )
+        for half, cols in enumerate(HALVES):
+            variance = psum.tile([P, N // 2], F32, name=f"variance{half}", tag="bank")
+            for cb in range(CB):
+                nc.vector.tensor_tensor(centred[cb][:, cols], h[cb][:, cols], mean[half][:], SUBTRACT)
+                nc.scalar.activation(squared[cb][:, cols], centred[cb][:, cols], SQUARE)
+                nc.tensor.matmul(
+                    variance[:], averager[:], squared[cb][:, cols],
+                    start=(cb == 0), stop=(cb == CB - 1),
+                )
+            nc.scalar.activation(rstd[:, cols], variance[:], RSQRT, bias=eps[:])
+            for cb in range(CB):
+                unit = work.tile([P, N // 2], F32, name="unit")
+                nc.vector.tensor_tensor(unit[:], centred[cb][:, cols], rstd[:, cols], MULT)
+                nc.scalar.activation(
+                    hn[cb][:, cols], unit[:], IDENTITY,
+                    bias=bias[:, cb : cb + 1], scale=gain[:, cb : cb + 1],
+                )
 
-        for blocks in [range(GROUP)] + [range(vb, vb + 1) for vb in range(GROUP, VB)]:
-            logits = {vb: psum.tile([P, N], F32, name=f"logits{vb}", tag="bank") for vb in blocks}
+        jobs = [(range(GROUP), cols) for cols in HALVES]
+        jobs += [(range(vb, vb + 1), WHOLE) for vb in range(GROUP, VB - 1)]
+        jobs += [(range(VB - 1, VB), cols) for cols in HALVES]
+        copies = 0
+        for blocks, cols in jobs:
+            width = hn[0][:, cols].shape[1]
+            logits = {vb: psum.tile([P, width], F32, name=f"logits{vb}", tag="bank") for vb in blocks}
             for cb in range(CB):
                 for vb in blocks:
                     nc.tensor.matmul(
-                        logits[vb][:], head[:, cb, vb * P : (vb + 1) * P], hn[cb][:],
+                        logits[vb][:], head[:, cb, vb * P : (vb + 1) * P], hn[cb][:, cols],
                         start=(cb == 0), stop=(cb == CB - 1),
                     )
             for vb in blocks:
-                staged = stage.tile([P, N], F32, name="staged")
-                if vb % 2 == 0:
+                staged = stage.tile([P, width], F32, name="staged")
+                if copies % 2 == 0:
                     nc.vector.tensor_copy(staged[:], logits[vb][:])
                 else:
                     nc.scalar.activation(staged[:], logits[vb][:], COPY)
-                nc.sync.dma_start(out[vb * P : (vb + 1) * P, :], staged[:])
+                copies += 1
+                nc.sync.dma_start(out[vb * P : (vb + 1) * P, cols], staged[:])

@@ -4,9 +4,11 @@ P = 128
 C, S, N = 512, 2048, 512
 CB = C // P
 VB = S // P
-GROUP = 4
-HALVES = (slice(0, N // 2), slice(N // 2, N))
-WHOLE = slice(0, N)
+LAST = CB - 1
+BOUNDS = (0, 128, 256, N)
+CHUNKS = len(BOUNDS) - 1
+PIECE = 4
+JOB = 256
 EPS = 1e-5
 FLOPS = 2 * C * S * N
 
@@ -23,86 +25,117 @@ def tile_tinygpt_ntp_kernel(tc, tok_emb, pos_emb, lnf_w, lnf_b, head_w, offs, ou
     with (
         tc.tile_pool(name="held", bufs=1) as held,
         tc.tile_pool(name="work", bufs=2) as work,
-        tc.tile_pool(name="stage", bufs=4) as stage,
+        tc.tile_pool(name="stage", bufs=10) as stage,
         tc.psum_pool(name="psum", bufs=8) as psum,
     ):
         offsets = held.tile([P, N // 16], U16, name="offsets")
         nc.sync.dma_start(offsets[:], offs)
-        tok = [held.tile([P, S], F32, name=f"tok{cb}") for cb in range(CB)]
-        pos = held.tile([P, CB, N], F32, name="pos")
-        head = held.tile([P, CB, S], BF16, name="head")
-        tok_blocks = tok_emb.rearrange("(p cb) s -> cb p s", cb=CB)
-        pos_blocks = pos_emb.rearrange("(p cb) j -> p cb j", cb=CB)
-        nc.sync.dma_start(pos[:, 0:1, :], pos_blocks[:, 0:1, :])
-        nc.sync.dma_start(tok[0][:], tok_blocks[0])
-        nc.sync.dma_start(pos[:, 1:CB, :], pos_blocks[:, 1:CB, :])
-        for cb in range(1, CB):
-            nc.sync.dma_start(tok[cb][:], tok_blocks[cb])
-        nc.sync.dma_start(head[:], head_w.rearrange("(p cb) v -> p cb v", cb=CB))
         gain = held.tile([P, CB], F32, name="gain")
         bias = held.tile([P, CB], F32, name="bias")
-        nc.sync.dma_start(gain[:], lnf_w.rearrange("(p cb) one -> p (cb one)", cb=CB))
-        nc.sync.dma_start(bias[:], lnf_b.rearrange("(p cb) one -> p (cb one)", cb=CB))
+        nc.scalar.dma_start(gain[:], lnf_w.rearrange("(p cb) one -> p (cb one)", cb=CB))
+        nc.scalar.dma_start(bias[:], lnf_b.rearrange("(p cb) one -> p (cb one)", cb=CB))
+        tok = [held.tile([P, S], F32, name=f"tok{cb}") for cb in range(CB)]
+        pos = [held.tile([P, N], F32, name=f"pos{cb}") for cb in range(CB)]
+        tok_blocks = tok_emb.rearrange("(p cb) s -> cb p s", cb=CB)
+        pos_blocks = pos_emb.rearrange("(p cb) j -> cb p j", cb=CB)
+        for cb in range(CB):
+            nc.sync.dma_start(pos[cb][:], pos_blocks[cb])
+            nc.sync.dma_start(tok[cb][:], tok_blocks[cb])
+        head_blocks = head_w.rearrange("(p cb) v -> p cb v", cb=CB)
+        head = [held.tile([P, CB, PIECE * P], BF16, name=f"head{g}") for g in range(VB // PIECE)]
+        for g in range(VB // PIECE):
+            nc.sync.dma_start(head[g][:], head_blocks[:, :, g * PIECE * P : (g + 1) * PIECE * P])
 
         averager = held.tile([P, P], F32, name="averager")
         nc.vector.memset(averager[:], 1.0 / C)
+        block_averager = held.tile([P, P], F32, name="block_averager")
+        nc.vector.memset(block_averager[:], 1.0 / P)
         eps = held.tile([P, 1], F32, name="eps")
         nc.vector.memset(eps[:], EPS)
         table_warmer = held.tile([P, 1], F32, name="table_warmer")
         nc.scalar.activation(table_warmer[:], eps[:], RSQRT)
 
-        mean = [psum.tile([P, N // 2], F32, name=f"mean{half}", tag="bank") for half in range(2)]
-        h = [held.tile([P, N], F32, name=f"h{cb}") for cb in range(CB)]
-        for cb in range(CB):
-            for half, cols in enumerate(HALVES):
-                entries = offsets[:, half * (N // 32) : (half + 1) * (N // 32)]
-                nc.vector.tensor_tensor(
-                    h[cb][:, cols], tok[cb][:].indirect(entries), pos[:, cb, cols], ADD
-                )
-                nc.tensor.matmul(
-                    mean[half][:], averager[:], h[cb][:, cols], start=(cb == 0), stop=(cb == CB - 1)
-                )
+        chunks = [slice(BOUNDS[k], BOUNDS[k + 1]) for k in range(CHUNKS)]
+        widths = [BOUNDS[k + 1] - BOUNDS[k] for k in range(CHUNKS)]
+        entries = [offsets[:, BOUNDS[k] // 16 : BOUNDS[k + 1] // 16] for k in range(CHUNKS)]
 
-        centred = [held.tile([P, N], F32, name=f"centred{cb}") for cb in range(CB)]
+        e = [held.tile([P, N], F32, name=f"e{cb}") for cb in range(CB)]
         squared = [held.tile([P, N], F32, name=f"squared{cb}") for cb in range(CB)]
-        rstd = held.tile([P, N], F32, name="rstd")
         hn = [held.tile([P, N], BF16, name=f"hn{cb}") for cb in range(CB)]
-        for half, cols in enumerate(HALVES):
-            variance = psum.tile([P, N // 2], F32, name=f"variance{half}", tag="bank")
-            for cb in range(CB):
-                nc.vector.tensor_tensor(centred[cb][:, cols], h[cb][:, cols], mean[half][:], SUBTRACT)
-                nc.scalar.activation(squared[cb][:, cols], centred[cb][:, cols], SQUARE)
+        mean_e = [psum.tile([P, widths[k]], F32, name=f"mean_e{k}", tag="bank") for k in range(CHUNKS)]
+        mean_ee = [psum.tile([P, widths[k]], F32, name=f"mean_ee{k}", tag="bank") for k in range(CHUNKS)]
+
+        def add_to_means(cb, k):
+            cols = chunks[k]
+            if cb > 0:
                 nc.tensor.matmul(
-                    variance[:], averager[:], squared[cb][:, cols],
-                    start=(cb == 0), stop=(cb == CB - 1),
+                    mean_e[k][:], averager[:], e[cb][:, cols], start=(cb == 1), stop=(cb == LAST)
                 )
-            nc.scalar.activation(rstd[:, cols], variance[:], RSQRT, bias=eps[:])
+            nc.scalar.activation(squared[cb][:, cols], e[cb][:, cols], SQUARE)
+            nc.tensor.matmul(
+                mean_ee[k][:], averager[:], squared[cb][:, cols], start=(cb == 0), stop=(cb == LAST)
+            )
+
+        h0 = held.tile([P, N], F32, name="h0")
+        shift = psum.tile([P, N], F32, name="shift", tag="bank")
+        for k, cols in enumerate(chunks):
+            nc.vector.tensor_tensor(h0[:, cols], tok[0][:].indirect(entries[k]), pos[0][:, cols], ADD)
+            nc.tensor.matmul(shift[:, cols], block_averager[:], h0[:, cols], start=True, stop=True)
+        for k, cols in enumerate(chunks):
+            nc.vector.tensor_tensor(e[0][:, cols], h0[:, cols], shift[:, cols], SUBTRACT)
+            add_to_means(0, k)
+
+        shifted_pos = [None] + [held.tile([P, N], F32, name=f"shifted_pos{cb}") for cb in range(1, CB)]
+
+        def look_up(cb, k):
+            cols = chunks[k]
+            nc.vector.tensor_tensor(
+                e[cb][:, cols], tok[cb][:].indirect(entries[k]), shifted_pos[cb][:, cols], ADD
+            )
+            add_to_means(cb, k)
+
+        for cb in range(1, CB):
+            nc.vector.tensor_tensor(shifted_pos[cb][:], pos[cb][:], shift[:], SUBTRACT)
+            if cb < LAST:
+                for k in range(CHUNKS):
+                    look_up(cb, k)
+
+        for k, cols in enumerate(chunks):
+            look_up(LAST, k)
+            mean_squared = work.tile([P, widths[k]], F32, name="mean_squared")
+            nc.scalar.activation(mean_squared[:], mean_e[k][:], SQUARE)
+            variance = work.tile([P, widths[k]], F32, name="variance")
+            nc.vector.tensor_tensor(variance[:], mean_ee[k][:], mean_squared[:], SUBTRACT)
+            rstd = work.tile([P, widths[k]], F32, name="rstd")
+            nc.scalar.activation(rstd[:], variance[:], RSQRT, bias=eps[:])
+            centred = [work.tile([P, widths[k]], F32, name=f"centred{cb}") for cb in range(CB)]
             for cb in range(CB):
-                unit = work.tile([P, N // 2], F32, name="unit")
-                nc.vector.tensor_tensor(unit[:], centred[cb][:, cols], rstd[:, cols], MULT)
+                nc.vector.tensor_tensor(centred[cb][:], e[cb][:, cols], mean_e[k][:], SUBTRACT)
+            for cb in range(CB):
+                unit = work.tile([P, widths[k]], F32, name=f"unit{cb}")
+                nc.vector.tensor_tensor(unit[:], centred[cb][:], rstd[:], MULT)
                 nc.scalar.activation(
                     hn[cb][:, cols], unit[:], IDENTITY,
                     bias=bias[:, cb : cb + 1], scale=gain[:, cb : cb + 1],
                 )
 
-        jobs = [(range(GROUP), cols) for cols in HALVES]
-        jobs += [(range(vb, vb + 1), WHOLE) for vb in range(GROUP, VB - 1)]
-        jobs += [(range(VB - 1, VB), cols) for cols in HALVES]
-        copies = 0
-        for blocks, cols in jobs:
-            width = hn[0][:, cols].shape[1]
-            logits = {vb: psum.tile([P, width], F32, name=f"logits{vb}", tag="bank") for vb in blocks}
-            for cb in range(CB):
-                for vb in blocks:
-                    nc.tensor.matmul(
-                        logits[vb][:], head[:, cb, vb * P : (vb + 1) * P], hn[cb][:, cols],
-                        start=(cb == 0), stop=(cb == CB - 1),
-                    )
-            for vb in blocks:
-                staged = stage.tile([P, width], F32, name="staged")
-                if copies % 2 == 0:
-                    nc.vector.tensor_copy(staged[:], logits[vb][:])
+        out_blocks = out.rearrange("(vb p) j -> p vb j", p=P)
+        jobs = 0
+        for k, cols in enumerate(chunks):
+            blocks = JOB // widths[k]
+            for first in range(0, VB, blocks):
+                logits = psum.tile([P, blocks, widths[k]], F32, name="logits", tag="bank")
+                for i in range(blocks):
+                    piece, block = divmod(first + i, PIECE)
+                    for cb in range(CB):
+                        nc.tensor.matmul(
+                            logits[:, i, :], head[piece][:, cb, block * P : (block + 1) * P],
+                            hn[cb][:, cols], start=(cb == 0), stop=(cb == CB - 1),
+                        )
+                staged = stage.tile([P, blocks, widths[k]], F32, name="staged")
+                if jobs % 2 == 0:
+                    nc.vector.tensor_copy(staged[:], logits[:])
                 else:
-                    nc.scalar.activation(staged[:], logits[vb][:], COPY)
-                copies += 1
-                nc.sync.dma_start(out[vb * P : (vb + 1) * P, cols], staged[:])
+                    nc.scalar.activation(staged[:], logits[:], COPY)
+                jobs += 1
+                nc.sync.dma_start(out_blocks[:, first : first + blocks, cols], staged[:])

@@ -77,12 +77,16 @@ def tile_tinygpt_ntp_kernel(tc, tok_emb, pos_emb, lnf_w, lnf_b, head_w, offs, ou
             )
 
         h0 = held.tile([P, N], F32, name="h0")
-        shift = psum.tile([P, N], F32, name="shift", tag="bank")
+        shift_halves = [psum.tile([P, N // 2], F32, name=f"shift{half}", tag="bank") for half in range(2)]
+        shift = []
+        for k in range(CHUNKS):
+            half, lo = divmod(BOUNDS[k], N // 2)
+            shift.append(shift_halves[half][:, lo : lo + widths[k]])
         for k, cols in enumerate(chunks):
             nc.vector.tensor_tensor(h0[:, cols], tok[0][:].indirect(entries[k]), pos[0][:, cols], ADD)
-            nc.tensor.matmul(shift[:, cols], block_averager[:], h0[:, cols], start=True, stop=True)
+            nc.tensor.matmul(shift[k], block_averager[:], h0[:, cols], start=True, stop=True)
         for k, cols in enumerate(chunks):
-            nc.vector.tensor_tensor(e[0][:, cols], h0[:, cols], shift[:, cols], SUBTRACT)
+            nc.vector.tensor_tensor(e[0][:, cols], h0[:, cols], shift[k], SUBTRACT)
             add_to_means(0, k)
 
         shifted_pos = [None] + [held.tile([P, N], F32, name=f"shifted_pos{cb}") for cb in range(1, CB)]
@@ -95,7 +99,8 @@ def tile_tinygpt_ntp_kernel(tc, tok_emb, pos_emb, lnf_w, lnf_b, head_w, offs, ou
             add_to_means(cb, k)
 
         for cb in range(1, CB):
-            nc.vector.tensor_tensor(shifted_pos[cb][:], pos[cb][:], shift[:], SUBTRACT)
+            for k, cols in enumerate(chunks):
+                nc.vector.tensor_tensor(shifted_pos[cb][:, cols], pos[cb][:, cols], shift[k], SUBTRACT)
             if cb < LAST:
                 for k in range(CHUNKS):
                     look_up(cb, k)

@@ -8,7 +8,8 @@ LAST = CB - 1
 BOUNDS = (0, 128, 256, N)
 CHUNKS = len(BOUNDS) - 1
 PIECE = 4
-JOB = 256
+BANK = 512
+JOB = (BANK, BANK, BANK // 2)
 EPS = 1e-5
 FLOPS = 2 * C * S * N
 
@@ -127,7 +128,7 @@ def tile_tinygpt_ntp_kernel(tc, tok_emb, pos_emb, lnf_w, lnf_b, head_w, offs, ou
         out_blocks = out.rearrange("(vb p) j -> p vb j", p=P)
         jobs = 0
         for k, cols in enumerate(chunks):
-            blocks = JOB // widths[k]
+            blocks = JOB[k] // widths[k]
             for first in range(0, VB, blocks):
                 logits = psum.tile([P, blocks, widths[k]], F32, name="logits", tag="bank")
                 for i in range(blocks):

@@ -8,8 +8,6 @@ LAST = CB - 1
 BOUNDS = (0, 128, 256, N)
 CHUNKS = len(BOUNDS) - 1
 PIECE = 4
-BANK = 512
-JOB = (BANK, BANK, BANK // 2)
 EPS = 1e-5
 FLOPS = 2 * C * S * N
 
@@ -125,23 +123,24 @@ def tile_tinygpt_ntp_kernel(tc, tok_emb, pos_emb, lnf_w, lnf_b, head_w, offs, ou
                     bias=bias[:, cb : cb + 1], scale=gain[:, cb : cb + 1],
                 )
 
+        both = slice(BOUNDS[0], BOUNDS[2])
+        jobs = [(0, PIECE, chunks[0]), (0, PIECE, chunks[1])]
+        jobs += [(first, 2, both) for first in range(PIECE, VB, 2)]
+        jobs += [(first, 1, chunks[2]) for first in range(VB)]
         out_blocks = out.rearrange("(vb p) j -> p vb j", p=P)
-        jobs = 0
-        for k, cols in enumerate(chunks):
-            blocks = JOB[k] // widths[k]
-            for first in range(0, VB, blocks):
-                logits = psum.tile([P, blocks, widths[k]], F32, name="logits", tag="bank")
-                for i in range(blocks):
-                    piece, block = divmod(first + i, PIECE)
-                    for cb in range(CB):
-                        nc.tensor.matmul(
-                            logits[:, i, :], head[piece][:, cb, block * P : (block + 1) * P],
-                            hn[cb][:, cols], start=(cb == 0), stop=(cb == CB - 1),
-                        )
-                staged = stage.tile([P, blocks, widths[k]], F32, name="staged")
-                if jobs % 2 == 0:
-                    nc.vector.tensor_copy(staged[:], logits[:])
-                else:
-                    nc.scalar.activation(staged[:], logits[:], COPY)
-                jobs += 1
-                nc.sync.dma_start(out_blocks[:, first : first + blocks, cols], staged[:])
+        for number, (first, blocks, cols) in enumerate(jobs):
+            width = cols.stop - cols.start
+            logits = psum.tile([P, blocks, width], F32, name="logits", tag="bank")
+            for i in range(blocks):
+                piece, block = divmod(first + i, PIECE)
+                for cb in range(CB):
+                    nc.tensor.matmul(
+                        logits[:, i, :], head[piece][:, cb, block * P : (block + 1) * P],
+                        hn[cb][:, cols], start=(cb == 0), stop=(cb == CB - 1),
+                    )
+            staged = stage.tile([P, blocks, width], F32, name="staged")
+            if number % 2 == 0:
+                nc.vector.tensor_copy(staged[:], logits[:])
+            else:
+                nc.scalar.activation(staged[:], logits[:], COPY)
+            nc.sync.dma_start(out_blocks[:, first : first + blocks, cols], staged[:])

@@ -126,7 +126,9 @@ def tile_tinygpt_ntp_kernel(tc, tok_emb, pos_emb, lnf_w, lnf_b, head_w, offs, ou
         both = slice(BOUNDS[0], BOUNDS[2])
         jobs = [(0, PIECE, chunks[0]), (0, PIECE, chunks[1])]
         jobs += [(first, 2, both) for first in range(PIECE, VB, 2)]
-        jobs += [(first, 1, chunks[2]) for first in range(VB)]
+        jobs += [(first, 1, chunks[2]) for first in range(VB - 1)]
+        middle = (BOUNDS[2] + BOUNDS[3]) // 2
+        jobs += [(VB - 1, 1, slice(BOUNDS[2], middle)), (VB - 1, 1, slice(middle, BOUNDS[3]))]
         out_blocks = out.rearrange("(vb p) j -> p vb j", p=P)
         for number, (first, blocks, cols) in enumerate(jobs):
             width = cols.stop - cols.start

@@ -29,10 +29,6 @@ def tile_tinygpt_ntp_kernel(tc, tok_emb, pos_emb, lnf_w, lnf_b, head_w, offs, ou
     ):
         offsets = held.tile([P, N // 16], U16, name="offsets")
         nc.sync.dma_start(offsets[:], offs)
-        gain = held.tile([P, CB], F32, name="gain")
-        bias = held.tile([P, CB], F32, name="bias")
-        nc.scalar.dma_start(gain[:], lnf_w.rearrange("(p cb) one -> p (cb one)", cb=CB))
-        nc.scalar.dma_start(bias[:], lnf_b.rearrange("(p cb) one -> p (cb one)", cb=CB))
         tok = [held.tile([P, S], F32, name=f"tok{cb}") for cb in range(CB)]
         pos = [held.tile([P, N], F32, name=f"pos{cb}") for cb in range(CB)]
         tok_blocks = tok_emb.rearrange("(p cb) s -> cb p s", cb=CB)
@@ -40,6 +36,10 @@ def tile_tinygpt_ntp_kernel(tc, tok_emb, pos_emb, lnf_w, lnf_b, head_w, offs, ou
         for cb in range(CB):
             nc.sync.dma_start(pos[cb][:], pos_blocks[cb])
             nc.sync.dma_start(tok[cb][:], tok_blocks[cb])
+        gain = held.tile([P, CB], F32, name="gain")
+        bias = held.tile([P, CB], F32, name="bias")
+        nc.sync.dma_start(gain[:], lnf_w.rearrange("(p cb) one -> p (cb one)", cb=CB))
+        nc.sync.dma_start(bias[:], lnf_b.rearrange("(p cb) one -> p (cb one)", cb=CB))
         head_blocks = head_w.rearrange("(p cb) v -> p cb v", cb=CB)
         head = [held.tile([P, CB, PIECE * P], BF16, name=f"head{g}") for g in range(VB // PIECE)]
         for g in range(VB // PIECE):

@@ -33,9 +33,11 @@ def tile_tinygpt_ntp_kernel(tc, tok_emb, pos_emb, lnf_w, lnf_b, head_w, offs, ou
         pos = [held.tile([P, N], F32, name=f"pos{cb}") for cb in range(CB)]
         tok_blocks = tok_emb.rearrange("(p cb) s -> cb p s", cb=CB)
         pos_blocks = pos_emb.rearrange("(p cb) j -> cb p j", cb=CB)
+        first_chunks, last_chunk = slice(BOUNDS[0], BOUNDS[CHUNKS - 1]), slice(BOUNDS[CHUNKS - 1], N)
         for cb in range(CB):
-            nc.sync.dma_start(pos[cb][:], pos_blocks[cb])
+            nc.sync.dma_start(pos[cb][:, first_chunks], pos_blocks[cb][:, first_chunks])
             nc.sync.dma_start(tok[cb][:], tok_blocks[cb])
+            nc.sync.dma_start(pos[cb][:, last_chunk], pos_blocks[cb][:, last_chunk])
         gain = held.tile([P, CB], F32, name="gain")
         bias = held.tile([P, CB], F32, name="bias")
         nc.sync.dma_start(gain[:], lnf_w.rearrange("(p cb) one -> p (cb one)", cb=CB))
@@ -84,7 +86,9 @@ def tile_tinygpt_ntp_kernel(tc, tok_emb, pos_emb, lnf_w, lnf_b, head_w, offs, ou
         for k, cols in enumerate(chunks):
             nc.vector.tensor_tensor(h0[:, cols], tok[0][:].indirect(entries[k]), pos[0][:, cols], ADD)
             nc.tensor.matmul(shift[k], block_averager[:], h0[:, cols], start=True, stop=True)
-        for k, cols in enumerate(chunks):
+
+        def take_shift_off_block_0(k):
+            cols = chunks[k]
             nc.vector.tensor_tensor(e[0][:, cols], h0[:, cols], shift[k], SUBTRACT)
             add_to_means(0, k)
 
@@ -97,9 +101,21 @@ def tile_tinygpt_ntp_kernel(tc, tok_emb, pos_emb, lnf_w, lnf_b, head_w, offs, ou
             )
             add_to_means(cb, k)
 
-        for cb in range(1, CB):
-            for k, cols in enumerate(chunks):
-                nc.vector.tensor_tensor(shifted_pos[cb][:, cols], pos[cb][:, cols], shift[k], SUBTRACT)
+        def take_shift_off_pos(cb, k):
+            cols = chunks[k]
+            nc.vector.tensor_tensor(shifted_pos[cb][:, cols], pos[cb][:, cols], shift[k], SUBTRACT)
+
+        for k in range(CHUNKS - 1):
+            take_shift_off_block_0(k)
+            take_shift_off_pos(1, k)
+        for k in range(CHUNKS - 1):
+            look_up(1, k)
+        take_shift_off_block_0(CHUNKS - 1)
+        take_shift_off_pos(1, CHUNKS - 1)
+        look_up(1, CHUNKS - 1)
+        for cb in range(2, CB):
+            for k in range(CHUNKS):
+                take_shift_off_pos(cb, k)
             if cb < LAST:
                 for k in range(CHUNKS):
                     look_up(cb, k)

@@ -140,12 +140,26 @@ def tile_tinygpt_ntp_kernel(tc, tok_emb, pos_emb, lnf_w, lnf_b, head_w, offs, ou
                 )
 
         both = slice(BOUNDS[0], BOUNDS[2])
-        jobs = [(0, PIECE, chunks[0]), (0, PIECE, chunks[1])]
+        jobs = [(0, PIECE, chunks[1])]
         jobs += [(first, 2, both) for first in range(PIECE, VB, 2)]
         jobs += [(first, 1, chunks[2]) for first in range(VB - 1)]
         middle = (BOUNDS[2] + BOUNDS[3]) // 2
         jobs += [(VB - 1, 1, slice(BOUNDS[2], middle)), (VB - 1, 1, slice(middle, BOUNDS[3]))]
         out_blocks = out.rearrange("(vb p) j -> p vb j", p=P)
+        first_logits = [psum.tile([P, widths[0]], F32, name=f"first_logits{i}", tag="bank") for i in range(PIECE)]
+        for cb in range(CB):
+            for i in range(PIECE):
+                nc.tensor.matmul(
+                    first_logits[i][:], head[0][:, cb, i * P : (i + 1) * P],
+                    hn[cb][:, chunks[0]], start=(cb == 0), stop=(cb == CB - 1),
+                )
+        first_staged = stage.tile([P, PIECE, widths[0]], F32, name="staged")
+        for i in range(PIECE):
+            if i % 2 == 0:
+                nc.vector.tensor_copy(first_staged[:, i, :], first_logits[i][:])
+            else:
+                nc.scalar.activation(first_staged[:, i, :], first_logits[i][:], COPY)
+        nc.sync.dma_start(out_blocks[:, 0:PIECE, chunks[0]], first_staged[:])
         for number, (first, blocks, cols) in enumerate(jobs):
             width = cols.stop - cols.start
             logits = psum.tile([P, blocks, width], F32, name="logits", tag="bank")

import concourse.mybir as mybir

P = 128
C, S, N = 512, 2048, 512
CB = C // P
VB = S // P
LAST = CB - 1
BOUNDS = (0, 128, 256, N)
CHUNKS = len(BOUNDS) - 1
PIECE = 4
EPS = 1e-5
FLOPS = 2 * C * S * N

F32, BF16, U16 = mybir.dt.float32, mybir.dt.bfloat16, mybir.dt.uint16
ADD, SUBTRACT, MULT = mybir.AluOpType.add, mybir.AluOpType.subtract, mybir.AluOpType.mult
SQUARE = mybir.ActivationFunctionType.Square
RSQRT = mybir.ActivationFunctionType.Abs_reciprocal_sqrt
IDENTITY = mybir.ActivationFunctionType.Identity
COPY = mybir.ActivationFunctionType.Copy


def tile_tinygpt_ntp_kernel(tc, tok_emb, pos_emb, lnf_w, lnf_b, head_w, offs, out):
    nc = tc.nc
    with (
        tc.tile_pool(name="held", bufs=1) as held,
        tc.tile_pool(name="work", bufs=2) as work,
        tc.tile_pool(name="stage", bufs=10) as stage,
        tc.psum_pool(name="psum", bufs=8) as psum,
    ):
        offsets = held.tile([P, N // 16], U16, name="offsets")
        nc.sync.dma_start(offsets[:], offs)
        tok = [held.tile([P, S], F32, name=f"tok{cb}") for cb in range(CB)]
        pos = [held.tile([P, N], F32, name=f"pos{cb}") for cb in range(CB)]
        tok_blocks = tok_emb.rearrange("(p cb) s -> cb p s", cb=CB)
        pos_blocks = pos_emb.rearrange("(p cb) j -> cb p j", cb=CB)
        first_chunks, last_chunk = slice(BOUNDS[0], BOUNDS[CHUNKS - 1]), slice(BOUNDS[CHUNKS - 1], N)
        for cb in range(CB):
            nc.sync.dma_start(pos[cb][:, first_chunks], pos_blocks[cb][:, first_chunks])
            nc.sync.dma_start(tok[cb][:], tok_blocks[cb])
            nc.sync.dma_start(pos[cb][:, last_chunk], pos_blocks[cb][:, last_chunk])
        gain = held.tile([P, CB], F32, name="gain")
        bias = held.tile([P, CB], F32, name="bias")
        nc.sync.dma_start(gain[:], lnf_w.rearrange("(p cb) one -> p (cb one)", cb=CB))
        nc.sync.dma_start(bias[:], lnf_b.rearrange("(p cb) one -> p (cb one)", cb=CB))
        head_blocks = head_w.rearrange("(p cb) v -> p cb v", cb=CB)
        head = [held.tile([P, CB, PIECE * P], BF16, name=f"head{g}") for g in range(VB // PIECE)]
        for g in range(VB // PIECE):
            nc.sync.dma_start(head[g][:], head_blocks[:, :, g * PIECE * P : (g + 1) * PIECE * P])

        averager = held.tile([P, P], F32, name="averager")
        nc.vector.memset(averager[:], 1.0 / C)
        block_averager = held.tile([P, P], F32, name="block_averager")
        nc.vector.memset(block_averager[:], 1.0 / P)
        eps = held.tile([P, 1], F32, name="eps")
        nc.vector.memset(eps[:], EPS)
        table_warmer = held.tile([P, 1], F32, name="table_warmer")
        nc.scalar.activation(table_warmer[:], eps[:], RSQRT)

        chunks = [slice(BOUNDS[k], BOUNDS[k + 1]) for k in range(CHUNKS)]
        widths = [BOUNDS[k + 1] - BOUNDS[k] for k in range(CHUNKS)]
        entries = [offsets[:, BOUNDS[k] // 16 : BOUNDS[k + 1] // 16] for k in range(CHUNKS)]

        e = [held.tile([P, N], F32, name=f"e{cb}") for cb in range(CB)]
        squared = [held.tile([P, N], F32, name=f"squared{cb}") for cb in range(CB)]
        hn = [held.tile([P, N], BF16, name=f"hn{cb}") for cb in range(CB)]
        mean_e = [psum.tile([P, widths[k]], F32, name=f"mean_e{k}", tag="bank") for k in range(CHUNKS)]
        mean_ee = [psum.tile([P, widths[k]], F32, name=f"mean_ee{k}", tag="bank") for k in range(CHUNKS)]

        def add_to_means(cb, k):
            cols = chunks[k]
            if cb > 0:
                nc.tensor.matmul(
                    mean_e[k][:], averager[:], e[cb][:, cols], start=(cb == 1), stop=(cb == LAST)
                )
            nc.scalar.activation(squared[cb][:, cols], e[cb][:, cols], SQUARE)
            nc.tensor.matmul(
                mean_ee[k][:], averager[:], squared[cb][:, cols], start=(cb == 0), stop=(cb == LAST)
            )

        h0 = held.tile([P, N], F32, name="h0")
        shift_halves = [psum.tile([P, N // 2], F32, name=f"shift{half}", tag="bank") for half in range(2)]
        shift = []
        for k in range(CHUNKS):
            half, lo = divmod(BOUNDS[k], N // 2)
            shift.append(shift_halves[half][:, lo : lo + widths[k]])
        for k, cols in enumerate(chunks):
            nc.vector.tensor_tensor(h0[:, cols], tok[0][:].indirect(entries[k]), pos[0][:, cols], ADD)
            nc.tensor.matmul(shift[k], block_averager[:], h0[:, cols], start=True, stop=True)

        def take_shift_off_block_0(k):
            cols = chunks[k]
            nc.vector.tensor_tensor(e[0][:, cols], h0[:, cols], shift[k], SUBTRACT)
            add_to_means(0, k)

        shifted_pos = [None] + [held.tile([P, N], F32, name=f"shifted_pos{cb}") for cb in range(1, CB)]

        def look_up(cb, k):
            cols = chunks[k]
            nc.vector.tensor_tensor(
                e[cb][:, cols], tok[cb][:].indirect(entries[k]), shifted_pos[cb][:, cols], ADD
            )
            add_to_means(cb, k)

        def take_shift_off_pos(cb, k):
            cols = chunks[k]
            nc.vector.tensor_tensor(shifted_pos[cb][:, cols], pos[cb][:, cols], shift[k], SUBTRACT)

        for k in range(CHUNKS - 1):
            take_shift_off_block_0(k)
            take_shift_off_pos(1, k)
        for k in range(CHUNKS - 1):
            look_up(1, k)
        take_shift_off_block_0(CHUNKS - 1)
        take_shift_off_pos(1, CHUNKS - 1)
        look_up(1, CHUNKS - 1)
        for cb in range(2, CB):
            for k in range(CHUNKS):
                take_shift_off_pos(cb, k)
            if cb < LAST:
                for k in range(CHUNKS):
                    look_up(cb, k)

        for k, cols in enumerate(chunks):
            look_up(LAST, k)
            mean_squared = work.tile([P, widths[k]], F32, name="mean_squared")
            nc.scalar.activation(mean_squared[:], mean_e[k][:], SQUARE)
            variance = work.tile([P, widths[k]], F32, name="variance")
            nc.vector.tensor_tensor(variance[:], mean_ee[k][:], mean_squared[:], SUBTRACT)
            rstd = work.tile([P, widths[k]], F32, name="rstd")
            nc.scalar.activation(rstd[:], variance[:], RSQRT, bias=eps[:])
            centred = [work.tile([P, widths[k]], F32, name=f"centred{cb}") for cb in range(CB)]
            for cb in range(CB):
                nc.vector.tensor_tensor(centred[cb][:], e[cb][:, cols], mean_e[k][:], SUBTRACT)
            for cb in range(CB):
                unit = work.tile([P, widths[k]], F32, name=f"unit{cb}")
                nc.vector.tensor_tensor(unit[:], centred[cb][:], rstd[:], MULT)
                nc.scalar.activation(
                    hn[cb][:, cols], unit[:], IDENTITY,
                    bias=bias[:, cb : cb + 1], scale=gain[:, cb : cb + 1],
                )

        both = slice(BOUNDS[0], BOUNDS[2])
        jobs = [(0, PIECE, chunks[1])]
        jobs += [(first, 2, both) for first in range(PIECE, VB, 2)]
        jobs += [(first, 1, chunks[2]) for first in range(VB - 1)]
        middle = (BOUNDS[2] + BOUNDS[3]) // 2
        jobs += [(VB - 1, 1, slice(BOUNDS[2], middle)), (VB - 1, 1, slice(middle, BOUNDS[3]))]
        out_blocks = out.rearrange("(vb p) j -> p vb j", p=P)
        first_logits = [psum.tile([P, widths[0]], F32, name=f"first_logits{i}", tag="bank") for i in range(PIECE)]
        for cb in range(CB):
            for i in range(PIECE):
                nc.tensor.matmul(
                    first_logits[i][:], head[0][:, cb, i * P : (i + 1) * P],
                    hn[cb][:, chunks[0]], start=(cb == 0), stop=(cb == CB - 1),
                )
        first_staged = stage.tile([P, PIECE, widths[0]], F32, name="staged")
        for i in range(PIECE):
            if i % 2 == 0:
                nc.vector.tensor_copy(first_staged[:, i, :], first_logits[i][:])
            else:
                nc.scalar.activation(first_staged[:, i, :], first_logits[i][:], COPY)
        nc.sync.dma_start(out_blocks[:, 0:PIECE, chunks[0]], first_staged[:])
        for number, (first, blocks, cols) in enumerate(jobs):
            width = cols.stop - cols.start
            logits = psum.tile([P, blocks, width], F32, name="logits", tag="bank")
            for i in range(blocks):
                piece, block = divmod(first + i, PIECE)
                for cb in range(CB):
                    nc.tensor.matmul(
                        logits[:, i, :], head[piece][:, cb, block * P : (block + 1) * P],
                        hn[cb][:, cols], start=(cb == 0), stop=(cb == CB - 1),
                    )
            staged = stage.tile([P, blocks, width], F32, name="staged")
            if number % 2 == 0:
                nc.vector.tensor_copy(staged[:], logits[:])
            else:
                nc.scalar.activation(staged[:], logits[:], COPY)
            nc.sync.dma_start(out_blocks[:, first : first + blocks, cols], staged[:])
